import numpy as np
import ml_dtypes


def mxq(x, axis, fmt="e4m3"):
    dtype, down = {"e4m3": (ml_dtypes.float8_e4m3fn, 7), "e5m2": (ml_dtypes.float8_e5m2, 14)}[fmt]
    v = np.moveaxis(np.asarray(x, np.float32).astype(ml_dtypes.bfloat16).astype(np.float64), axis, -1)
    blocks = v.reshape(v.shape[:-1] + (-1, 32))
    amax = np.abs(blocks).max(-1, keepdims=True)
    byte = np.maximum(np.where(amax > 0, np.frexp(amax)[1] - 1 + 127, 0) - down, 1)
    scale = np.exp2(byte - 127.0)
    codes = (blocks / scale).astype(np.float32).astype(dtype).astype(np.float64)
    return np.moveaxis((codes * scale).reshape(v.shape), -1, axis)


WIDE = False


def mx_kscale(k):
    if not WIDE:
        return np.ones(k)
    levels = np.array([30, -30])
    if k % 512:
        return np.exp2(np.random.permutation(np.resize(levels, k // 32))).repeat(32)
    a = np.empty((k // 512, 16))
    for p in range(k // 512):
        a[p, :8] = np.random.permutation(np.resize(levels, 8))
        for g in range(8):
            far = levels[np.abs(levels - a[p, g]) >= 10]
            a[p, g + 8] = far[np.random.randint(len(far))]
    return np.exp2(a.ravel()).repeat(32)


BF16 = ml_dtypes.bfloat16


def bf(x):
    return np.asarray(x, np.float32).astype(BF16)


def f64(x):
    return np.asarray(x).astype(np.float64)


B, S, E, H = 2, 1024, 1024, 4
D = E // H
LN_EPS = 1e-6


def setup_inputs():
    s = mx_kscale(E)
    return {"h_attn": bf(np.random.standard_normal((B, H, S, D)) * 0.4 * s.reshape(H, 1, D)),
            "x": bf(np.random.standard_normal((B, S, E))),
            "out_w": bf(np.random.standard_normal((E, E)) * 2.0 / np.sqrt(E) / s[:, None]),
            "ln_gamma": bf(1.0 + 0.1 * np.random.standard_normal(E)),
            "ln_beta": bf(0.1 * np.random.standard_normal(E))}


def reference(h_attn, x, out_w, ln_gamma, ln_beta):
    merged = f64(h_attn).transpose(0, 2, 1, 3).reshape(B, S, E)
    out = mxq(merged, 2, "e5m2") @ mxq(f64(out_w), 0, "e5m2")
    y = out + f64(x)
    mean = y.mean(-1, keepdims=True)
    var = np.square(y - mean).mean(-1, keepdims=True)
    return (y - mean) / np.sqrt(var + LN_EPS) * f64(ln_gamma) + f64(ln_beta)

@@ -1,0 +1,301 @@
+from contextlib import ExitStack
+
+import concourse.mybir as mybir
+from concourse.masks import make_identity
+
+F32 = mybir.dt.float32
+BF16 = mybir.dt.bfloat16
+U32 = mybir.dt.uint32
+U8 = mybir.dt.uint8
+E5X4 = mybir.dt.float8_e5m2_x4
+ALU = mybir.AluOpType
+ACT = mybir.ActivationFunctionType
+
+P = 128
+E = 1024
+NT = 16
+HALF = 512
+LN_EPS = 1e-6
+
+FLOPS = 2 * 2048 * 1024 * 1024
+
+
+def cv_of(i):
+    return E if i == NT - 1 else HALF
+
+
+def tile_selfattention_pa_kernel(tc, h_attn, x, out_w, ln_gamma, ln_beta, out):
+    nc = tc.nc
+
+    x_v = x.flatten_outer_dims().rearrange("(r p j) e -> r p j e", p=P, j=2)
+    o_v = out.flatten_outer_dims().rearrange("(r p j) e -> r p j e", p=P, j=2)
+    h_v = h_attn.rearrange("b h (q p j) d -> b q j p h d", p=P, j=2)
+    w_v = out_w.rearrange("(g p t) n -> g p t n", p=P, t=4)
+
+    with ExitStack() as ctx:
+        const = ctx.enter_context(tc.tile_pool(name="const", bufs=1))
+        hpool = ctx.enter_context(tc.tile_pool(name="hpool", bufs=NT))
+        xpool = ctx.enter_context(tc.tile_pool(name="xpool", bufs=NT // 2))
+        wrpool = ctx.enter_context(tc.tile_pool(name="wrpool", bufs=4))
+        wgpool = ctx.enter_context(tc.tile_pool(name="wgpool", bufs=2))
+        gpool = ctx.enter_context(tc.tile_pool(name="gpool", bufs=2))
+        mqpool = ctx.enter_context(tc.tile_pool(name="mqpool", bufs=3))
+        ypool = ctx.enter_context(tc.tile_pool(name="ypool", bufs=4))
+        opool = ctx.enter_context(tc.tile_pool(name="opool", bufs=8))
+        spool = ctx.enter_context(tc.tile_pool(name="spool", bufs=6))
+        ps_gb = ctx.enter_context(tc.psum_pool(name="ps_gb", bufs=1))
+        ps_acc = ctx.enter_context(tc.psum_pool(name="ps_acc", bufs=4))
+        ps_t = ctx.enter_context(tc.psum_pool(name="ps_t", bufs=3))
+        ctx.enter_context(tc.manual_schedule())
+
+        w_raw = {}
+        hs = {}
+        xs = {}
+
+        def load_w(c):
+            half, g = divmod(c, 2)
+            t = wrpool.tile([P, 4, HALF], BF16, name="w_raw", tag="w_raw")
+            nc.sync.dma_start(out=t[:], in_=w_v[g][:, :, half * HALF:(half + 1) * HALF])
+            w_raw[c] = t
+
+        def load_h(i):
+            r, j = divmod(i, 2)
+            b, q = divmod(r, 4)
+            t = hpool.tile([P, E], BF16, name="hs", tag="hs")
+            nc.sync.dma_start(out=t[:].rearrange("p (h d) -> p h d", h=4), in_=h_v[b, q, j])
+            hs[i] = t
+
+        def load_x(r):
+            t = xpool.tile([P, 2, E], BF16, name="xs", tag="xs")
+            nc.sync.dma_start(out=t[:], in_=x_v[r])
+            xs[r] = t
+
+        gb_stage = const.tile([1, 2 * E], BF16, name="gb_stage")
+        nc.sync.dma_start(out=gb_stage[0:1, 0:E], in_=ln_gamma.rearrange("(o e) -> o e", o=1))
+        nc.sync.dma_start(out=gb_stage[0:1, E:2 * E], in_=ln_beta.rearrange("(o e) -> o e", o=1))
+        load_w(0)
+        load_w(1)
+        load_h(0)
+        load_h(1)
+        load_w(2)
+        load_w(3)
+        load_x(0)
+        for r in range(1, NT // 2):
+            load_h(2 * r)
+            load_h(2 * r + 1)
+            load_x(r)
+
+        gb_row = const.tile([P, 2 * E], BF16, name="gb_row")
+        nc.vector.memset(gb_row[:], 0.0)
+        ones = const.tile([P, P], BF16, name="ones")
+        nc.vector.memset(ones[:], 1.0)
+        warm = const.tile([P, 1], F32, name="warm")
+        nc.vector.memset(warm[:], 1.0)
+        ident = const.tile([P, P], F32, name="ident")
+        make_identity(nc, ident[:])
+        warm2 = const.tile([P, 1], F32, name="warm2")
+        nc.scalar.activation(out=warm2[:], in_=warm[:], func=ACT.Sqrt)
+        nc.scalar.copy(out=gb_row[0:1, :], in_=gb_stage[0:1, :])
+
+        gb_v = ps_gb.tile([P, 2 * HALF], BF16, name="gb_v")
+        gb_g = const.tile([P, 2 * HALF], F32, name="gb_g")
+        junk = const.tile([P, E], BF16, name="junk")
+        junk2 = const.tile([P, 2], F32, name="junk2")
+        w_codes = const.tile([P, 2, E], U32, name="w_codes", align_bytes=64)
+        w_scales = const.tile([P, 2, E], U8, name="w_scales", align_bytes=64)
+
+        def gb_bcast():
+            nc.tensor.matmul(out=gb_v[:, 0:HALF], lhsT=ones[:], rhs=gb_row[:, 0:HALF], start=True, stop=True)
+            nc.tensor.matmul(out=gb_v[:, HALF:E], lhsT=ones[:], rhs=gb_row[:, E:E + HALF], start=True, stop=True)
+            gb_gp = ps_t.tile([P, 2 * HALF], BF16, name="xt", tag="xt")
+            nc.tensor.matmul(out=gb_gp[:, 0:HALF], lhsT=ones[:], rhs=gb_row[:, HALF:E], start=True, stop=True)
+            nc.tensor.matmul(out=gb_gp[:, HALF:E], lhsT=ones[:], rhs=gb_row[:, E + HALF:2 * E], start=True, stop=True)
+            nc.scalar.copy(out=gb_g[:], in_=gb_gp[:])
+
+        w_grp = {}
+
+        def wcopy(c):
+            grp = wgpool.tile([P, HALF, 4], BF16, name="w_grp", tag="w_grp", align_bytes=64)
+            src = w_raw[c][:].rearrange("p t n -> p n t")
+            nc.vector.tensor_copy(out=grp[:, 0:256, :], in_=src[:, 0:256, :])
+            nc.scalar.copy(out=grp[:, 256:HALF, :], in_=src[:, 256:HALF, :])
+            w_grp[c] = grp
+
+        def wq(c):
+            half, g = divmod(c, 2)
+            cols = slice(half * HALF, (half + 1) * HALF)
+            nc.vector.quantize_mx(
+                out=w_codes[:, g, cols].bitcast(E5X4),
+                scales=w_scales[:, g, cols],
+                in_=w_grp[c][:].rearrange("p n t -> p (n t)"),
+            )
+
+        m_grp = {}
+        m_q = {}
+        xts = {}
+
+        def trp(i):
+            words = hs[i][:].bitcast(F32)
+            xt = ps_t.tile([P, HALF], F32, name="xt", tag="xt")
+            for g in range(2):
+                for u in range(2):
+                    nc.tensor.transpose(
+                        xt[:, (2 * g + u) * P:(2 * g + u + 1) * P],
+                        words[:, 256 * g + u:256 * (g + 1):2],
+                        ident[:],
+                    )
+            xts[i] = xt
+
+        def cpo(i):
+            pair, s = divmod(i, 2)
+            if s == 0:
+                m_grp[pair] = gpool.tile([P, 2 * E], BF16, name="m_grp", tag="m_grp", align_bytes=64)
+            dst = m_grp[pair][:, s * E:(s + 1) * E].bitcast(F32).rearrange("p (g r u) -> p g r u", g=2, u=2)
+            nc.scalar.copy(out=dst, in_=xts[i][:].rearrange("p (g u r) -> p g r u", g=2, u=2))
+
+        def quant(pair):
+            mc = mqpool.tile([P, HALF], U32, name="mc", tag="mc", align_bytes=64)
+            ms = mqpool.tile([P, HALF], U8, name="ms", tag="ms", align_bytes=64)
+            nc.vector.quantize_mx(out=mc[:].bitcast(E5X4), scales=ms[:], in_=m_grp[pair][:])
+            m_q[pair] = (mc, ms)
+
+        accs = {}
+        ys = {}
+        os_ = {}
+        sts = {}
+
+        def mmh(i, half):
+            pair, s = divmod(i, 2)
+            mc, ms = m_q[pair]
+            acc = ps_acc.tile([P, HALF], F32, name="acc", tag="acc")
+            cols = slice(half * HALF, (half + 1) * HALF)
+            for g in range(2):
+                mcols = slice(s * 256 + g * P, s * 256 + (g + 1) * P)
+                nc.tensor.matmul_mx(
+                    out=acc[:],
+                    lhsT=mc[:, mcols].bitcast(E5X4),
+                    lhsT_scale=ms[:, mcols],
+                    rhs=w_codes[:, g, cols].bitcast(E5X4),
+                    rhs_scale=w_scales[:, g, cols],
+                    start=(g == 0),
+                    stop=(g == 1),
+                )
+            accs[(i, half)] = acc
+
+        def add_x(i, half):
+            r, j = divmod(i, 2)
+            if half == 0:
+                ys[i] = ypool.tile([P, E], F32, name="y", tag="y")
+                sts[i] = spool.tile([P, 8], F32, name="st", tag="st")
+            cols = slice(half * HALF, (half + 1) * HALF)
+            nc.vector.scalar_tensor_tensor(
+                out=ys[i][:, cols], in0=accs[(i, half)][:], scalar=1.0, in1=xs[r][:, j, cols],
+                op0=ALU.mult, op1=ALU.add, accum_out=sts[i][:, half:half + 1],
+            )
+
+        def negmean(i):
+            st = sts[i]
+            nc.scalar.activation(out=junk2[:], in_=st[:, 0:2], func=ACT.Identity, scale=-1.0 / E,
+                                 accum_out=st[:, 2:3])
+
+        def sumsq(i):
+            st = sts[i]
+            nc.scalar.activation(out=junk[:], in_=ys[i][:], func=ACT.Square, bias=st[:, 2:3], scale=1.0,
+                                 accum_out=st[:, 3:4])
+            nc.scalar.activation(out=st[:, 4:5], in_=st[:, 3:4], func=ACT.Sqrt, scale=1.0 / E, bias=LN_EPS)
+
+        def recip(i):
+            st = sts[i]
+            nc.vector.reciprocal(out=st[:, 5:6], in_=st[:, 4:5])
+
+        def t1(i):
+            o = opool.tile([P, E], F32, name="o", tag="o")
+            os_[i] = o
+            nc.vector.scalar_tensor_tensor(
+                out=o[:, 0:HALF], in0=ys[i][:, 0:HALF], scalar=sts[i][:, 2:3], in1=gb_v[:, 0:HALF],
+                op0=ALU.add, op1=ALU.mult,
+            )
+            if cv_of(i) == E:
+                nc.vector.scalar_tensor_tensor(
+                    out=o[:, HALF:E], in0=ys[i][:, HALF:E], scalar=sts[i][:, 2:3], in1=gb_g[:, 0:HALF],
+                    op0=ALU.add, op1=ALU.mult,
+                )
+
+        def t2(i):
+            o = os_[i]
+            nc.vector.scalar_tensor_tensor(
+                out=o[:, 0:HALF], in0=o[:, 0:HALF], scalar=sts[i][:, 5:6], in1=gb_v[:, HALF:E],
+                op0=ALU.mult, op1=ALU.add,
+            )
+            if cv_of(i) == E:
+                nc.vector.scalar_tensor_tensor(
+                    out=o[:, HALF:E], in0=o[:, HALF:E], scalar=sts[i][:, 5:6], in1=gb_g[:, HALF:E],
+                    op0=ALU.mult, op1=ALU.add,
+                )
+
+        def zg(i):
+            if cv_of(i) == E:
+                return
+            st, o = sts[i], os_[i]
+            nc.scalar.activation(out=st[:, 6:7], in_=st[:, 2:3], func=ACT.Identity, scale=st[:, 5:6])
+            nc.scalar.activation(out=o[:, HALF:E], in_=ys[i][:, HALF:E], func=ACT.Identity,
+                                 scale=st[:, 5:6], bias=st[:, 6:7])
+            nc.gpsimd.tensor_tensor(out=o[:, HALF:E], in0=o[:, HALF:E], in1=gb_g[:, 0:HALF], op=ALU.mult)
+            nc.gpsimd.tensor_tensor(out=o[:, HALF:E], in0=o[:, HALF:E], in1=gb_g[:, HALF:E], op=ALU.add)
+
+        def store(i):
+            r, j = divmod(i, 2)
+            nc.sync.dma_start(out=o_v[r][:, j, :], in_=os_[i][:])
+
+        wcopy(0)
+        wcopy(1)
+        wq(0)
+        wq(1)
+        trp(0)
+        trp(1)
+        cpo(0)
+        cpo(1)
+        wcopy(2)
+        quant(0)
+        wcopy(3)
+        wq(2)
+        gb_bcast()
+        mmh(0, 0)
+        mmh(1, 0)
+        wq(3)
+        mmh(0, 1)
+        mmh(1, 1)
+        trp(2)
+        trp(3)
+
+        for k in range(NT + 1):
+            if k < NT:
+                add_x(k, 0)
+            if k >= 1:
+                recip(k - 1)
+            if k < NT:
+                add_x(k, 1)
+            if k == 1:
+                quant(1)
+            if k >= 2 and k % 2 == 0 and k + 3 < NT:
+                quant(k // 2 + 1)
+            if k >= 1:
+                zg(k - 1)
+                t2(k - 1)
+                store(k - 1)
+            if k < NT:
+                negmean(k)
+                t1(k)
+                sumsq(k)
+            if k == 0:
+                cpo(2)
+                cpo(3)
+            if k + 4 < NT:
+                trp(k + 4)
+                cpo(k + 4)
+            if k == 1:
+                mmh(2, 0)
+                mmh(2, 1)
+            if k >= 1 and k + 2 < NT:
+                mmh(k + 2, 0)
+                mmh(k + 2, 1)

@@ -16,12 +16,16 @@ E = 1024
 NT = 16
 HALF = 512
 LN_EPS = 1e-6
-
-FLOPS = 2 * 2048 * 1024 * 1024
+WV = 336
+LOOK = 5
+CV_MAIN = 560
+CV_LAST = (768, 1024)
 
 
 def cv_of(i):
-    return E if i == NT - 1 else HALF
+    return CV_MAIN if i < NT - 2 else CV_LAST[i - (NT - 2)]
+
+FLOPS = 2 * 2048 * 1024 * 1024
 
 
 def tile_selfattention_pa_kernel(tc, h_attn, x, out_w, ln_gamma, ln_beta, out):
@@ -38,14 +42,14 @@ def tile_selfattention_pa_kernel(tc, h_attn, x, out_w, ln_gamma, ln_beta, out):
         xpool = ctx.enter_context(tc.tile_pool(name="xpool", bufs=NT // 2))
         wrpool = ctx.enter_context(tc.tile_pool(name="wrpool", bufs=4))
         wgpool = ctx.enter_context(tc.tile_pool(name="wgpool", bufs=2))
-        gpool = ctx.enter_context(tc.tile_pool(name="gpool", bufs=2))
-        mqpool = ctx.enter_context(tc.tile_pool(name="mqpool", bufs=3))
-        ypool = ctx.enter_context(tc.tile_pool(name="ypool", bufs=4))
-        opool = ctx.enter_context(tc.tile_pool(name="opool", bufs=8))
-        spool = ctx.enter_context(tc.tile_pool(name="spool", bufs=6))
+        gpool = ctx.enter_context(tc.tile_pool(name="gpool", bufs=3))
+        mqpool = ctx.enter_context(tc.tile_pool(name="mqpool", bufs=4))
+        ypool = ctx.enter_context(tc.tile_pool(name="ypool", bufs=5))
+        opool = ctx.enter_context(tc.tile_pool(name="opool", bufs=9))
+        spool = ctx.enter_context(tc.tile_pool(name="spool", bufs=8))
         ps_gb = ctx.enter_context(tc.psum_pool(name="ps_gb", bufs=1))
         ps_acc = ctx.enter_context(tc.psum_pool(name="ps_acc", bufs=4))
-        ps_t = ctx.enter_context(tc.psum_pool(name="ps_t", bufs=3))
+        ps_t = ctx.enter_context(tc.psum_pool(name="ps_t", bufs=2))
         ctx.enter_context(tc.manual_schedule())
 
         w_raw = {}
@@ -65,10 +69,8 @@ def tile_selfattention_pa_kernel(tc, h_attn, x, out_w, ln_gamma, ln_beta, out):
             nc.sync.dma_start(out=t[:].rearrange("p (h d) -> p h d", h=4), in_=h_v[b, q, j])
             hs[i] = t
 
-        def load_x(r):
-            t = xpool.tile([P, 2, E], BF16, name="xs", tag="xs")
-            nc.sync.dma_start(out=t[:], in_=x_v[r])
-            xs[r] = t
+        def new_x(r):
+            xs[r] = xpool.tile([P, 2, E], BF16, name="xs", tag="xs")
 
         gb_stage = const.tile([1, 2 * E], BF16, name="gb_stage")
         nc.sync.dma_start(out=gb_stage[0:1, 0:E], in_=ln_gamma.rearrange("(o e) -> o e", o=1))
@@ -76,14 +78,17 @@ def tile_selfattention_pa_kernel(tc, h_attn, x, out_w, ln_gamma, ln_beta, out):
         load_w(0)
         load_w(1)
         load_h(0)
-        load_h(1)
         load_w(2)
         load_w(3)
-        load_x(0)
+        new_x(0)
+        nc.sync.dma_start(out=xs[0][:, 0, :], in_=x_v[0][:, 0, :])
+        load_h(1)
+        nc.sync.dma_start(out=xs[0][:, 1, :], in_=x_v[0][:, 1, :])
         for r in range(1, NT // 2):
             load_h(2 * r)
             load_h(2 * r + 1)
-            load_x(r)
+            new_x(r)
+            nc.sync.dma_start(out=xs[r][:], in_=x_v[r])
 
         gb_row = const.tile([P, 2 * E], BF16, name="gb_row")
         nc.vector.memset(gb_row[:], 0.0)
@@ -94,31 +99,38 @@ def tile_selfattention_pa_kernel(tc, h_attn, x, out_w, ln_gamma, ln_beta, out):
         ident = const.tile([P, P], F32, name="ident")
         make_identity(nc, ident[:])
         warm2 = const.tile([P, 1], F32, name="warm2")
-        nc.scalar.activation(out=warm2[:], in_=warm[:], func=ACT.Sqrt)
+        nc.scalar.activation(out=warm2[:], in_=warm[:], func=ACT.Abs_reciprocal_sqrt)
         nc.scalar.copy(out=gb_row[0:1, :], in_=gb_stage[0:1, :])
 
-        gb_v = ps_gb.tile([P, 2 * HALF], BF16, name="gb_v")
-        gb_g = const.tile([P, 2 * HALF], F32, name="gb_g")
+        gam_ps = ps_gb.tile([P, E], BF16, name="gam_ps")
+        bet_ps = ps_gb.tile([P, E], BF16, name="bet_ps")
+        gam_sb = const.tile([P, E], BF16, name="gam_sb")
+        bet_sb = const.tile([P, E], BF16, name="bet_sb")
         junk = const.tile([P, E], BF16, name="junk")
         junk2 = const.tile([P, 2], F32, name="junk2")
         w_codes = const.tile([P, 2, E], U32, name="w_codes", align_bytes=64)
         w_scales = const.tile([P, 2, E], U8, name="w_scales", align_bytes=64)
 
         def gb_bcast():
-            nc.tensor.matmul(out=gb_v[:, 0:HALF], lhsT=ones[:], rhs=gb_row[:, 0:HALF], start=True, stop=True)
-            nc.tensor.matmul(out=gb_v[:, HALF:E], lhsT=ones[:], rhs=gb_row[:, E:E + HALF], start=True, stop=True)
-            gb_gp = ps_t.tile([P, 2 * HALF], BF16, name="xt", tag="xt")
-            nc.tensor.matmul(out=gb_gp[:, 0:HALF], lhsT=ones[:], rhs=gb_row[:, HALF:E], start=True, stop=True)
-            nc.tensor.matmul(out=gb_gp[:, HALF:E], lhsT=ones[:], rhs=gb_row[:, E + HALF:2 * E], start=True, stop=True)
-            nc.scalar.copy(out=gb_g[:], in_=gb_gp[:])
+            for half in range(2):
+                cols = slice(half * HALF, (half + 1) * HALF)
+                nc.tensor.matmul(out=gam_ps[:, cols], lhsT=ones[:], rhs=gb_row[:, cols], start=True, stop=True)
+            for half in range(2):
+                cols = slice(half * HALF, (half + 1) * HALF)
+                nc.tensor.matmul(out=bet_ps[:, cols], lhsT=ones[:], rhs=gb_row[:, E + half * HALF:E + (half + 1) * HALF],
+                                 start=True, stop=True)
+
+        def gb_copy():
+            nc.scalar.copy(out=gam_sb[:, CV_MAIN:E], in_=gam_ps[:, CV_MAIN:E])
+            nc.scalar.copy(out=bet_sb[:, CV_MAIN:E], in_=bet_ps[:, CV_MAIN:E])
 
         w_grp = {}
 
         def wcopy(c):
             grp = wgpool.tile([P, HALF, 4], BF16, name="w_grp", tag="w_grp", align_bytes=64)
             src = w_raw[c][:].rearrange("p t n -> p n t")
-            nc.vector.tensor_copy(out=grp[:, 0:256, :], in_=src[:, 0:256, :])
-            nc.scalar.copy(out=grp[:, 256:HALF, :], in_=src[:, 256:HALF, :])
+            nc.vector.tensor_copy(out=grp[:, 0:WV, :], in_=src[:, 0:WV, :])
+            nc.scalar.copy(out=grp[:, WV:HALF, :], in_=src[:, WV:HALF, :])
             w_grp[c] = grp
 
         def wq(c):
@@ -135,6 +147,8 @@ def tile_selfattention_pa_kernel(tc, h_attn, x, out_w, ln_gamma, ln_beta, out):
         xts = {}
 
         def trp(i):
+            if i >= NT:
+                return
             words = hs[i][:].bitcast(F32)
             xt = ps_t.tile([P, HALF], F32, name="xt", tag="xt")
             for g in range(2):
@@ -147,17 +161,24 @@ def tile_selfattention_pa_kernel(tc, h_attn, x, out_w, ln_gamma, ln_beta, out):
             xts[i] = xt
 
         def cpo(i):
-            pair, s = divmod(i, 2)
-            if s == 0:
-                m_grp[pair] = gpool.tile([P, 2 * E], BF16, name="m_grp", tag="m_grp", align_bytes=64)
-            dst = m_grp[pair][:, s * E:(s + 1) * E].bitcast(F32).rearrange("p (g r u) -> p g r u", g=2, u=2)
+            if i >= NT:
+                return
+            if i < 2 or i % 2 == 0:
+                grp = gpool.tile([P, 2 * E], BF16, name="m_grp", tag="m_grp", align_bytes=64)
+                m_grp[i] = (grp, 0)
+                if i >= 2:
+                    m_grp[i + 1] = (grp, 1)
+            grp, s = m_grp[i]
+            dst = grp[:, s * E:(s + 1) * E].bitcast(F32).rearrange("p (g r u) -> p g r u", g=2, u=2)
             nc.scalar.copy(out=dst, in_=xts[i][:].rearrange("p (g u r) -> p g r u", g=2, u=2))
 
-        def quant(pair):
+        def quant(i, n):
             mc = mqpool.tile([P, HALF], U32, name="mc", tag="mc", align_bytes=64)
             ms = mqpool.tile([P, HALF], U8, name="ms", tag="ms", align_bytes=64)
-            nc.vector.quantize_mx(out=mc[:].bitcast(E5X4), scales=ms[:], in_=m_grp[pair][:])
-            m_q[pair] = (mc, ms)
+            grp = m_grp[i][0]
+            nc.vector.quantize_mx(out=mc[:, 0:n * 256].bitcast(E5X4), scales=ms[:, 0:n * 256], in_=grp[:, 0:n * E])
+            for s in range(n):
+                m_q[i + s] = (mc, ms, s)
 
         accs = {}
         ys = {}
@@ -165,8 +186,7 @@ def tile_selfattention_pa_kernel(tc, h_attn, x, out_w, ln_gamma, ln_beta, out):
         sts = {}
 
         def mmh(i, half):
-            pair, s = divmod(i, 2)
-            mc, ms = m_q[pair]
+            mc, ms, s = m_q[i]
             acc = ps_acc.tile([P, HALF], F32, name="acc", tag="acc")
             cols = slice(half * HALF, (half + 1) * HALF)
             for g in range(2):
@@ -181,6 +201,10 @@ def tile_selfattention_pa_kernel(tc, h_attn, x, out_w, ln_gamma, ln_beta, out):
                     stop=(g == 1),
                 )
             accs[(i, half)] = acc
+
+        def mm(i):
+            mmh(i, 0)
+            mmh(i, 1)
 
         def add_x(i, half):
             r, j = divmod(i, 2)
@@ -202,100 +226,132 @@ def tile_selfattention_pa_kernel(tc, h_attn, x, out_w, ln_gamma, ln_beta, out):
             st = sts[i]
             nc.scalar.activation(out=junk[:], in_=ys[i][:], func=ACT.Square, bias=st[:, 2:3], scale=1.0,
                                  accum_out=st[:, 3:4])
-            nc.scalar.activation(out=st[:, 4:5], in_=st[:, 3:4], func=ACT.Sqrt, scale=1.0 / E, bias=LN_EPS)
 
-        def recip(i):
+        def rstd(i):
             st = sts[i]
-            nc.vector.reciprocal(out=st[:, 5:6], in_=st[:, 4:5])
+            nc.scalar.activation(out=st[:, 5:6], in_=st[:, 3:4], func=ACT.Abs_reciprocal_sqrt,
+                                 scale=1.0 / E, bias=LN_EPS)
+
+        def new_o(i):
+            os_[i] = opool.tile([P, E], F32, name="o", tag="o")
+
+        def nmr(i):
+            st = sts[i]
+            nc.scalar.activation(out=st[:, 6:7], in_=st[:, 2:3], func=ACT.Identity, scale=st[:, 5:6])
+
+        def zs(i):
+            st, o, cv = sts[i], os_[i], cv_of(i)
+            nc.scalar.activation(out=o[:, cv:E], in_=ys[i][:, cv:E], func=ACT.Identity,
+                                 scale=st[:, 5:6], bias=st[:, 6:7])
+
+        def g1(i):
+            o, cv = os_[i], cv_of(i)
+            nc.gpsimd.tensor_tensor(out=o[:, cv:E], in0=o[:, cv:E], in1=gam_sb[:, cv:E], op=ALU.mult)
+
+        def g2(i):
+            o, cv = os_[i], cv_of(i)
+            nc.gpsimd.tensor_tensor(out=o[:, cv:E], in0=o[:, cv:E], in1=bet_sb[:, cv:E], op=ALU.add)
 
         def t1(i):
-            o = opool.tile([P, E], F32, name="o", tag="o")
-            os_[i] = o
+            o, cv = os_[i], cv_of(i)
             nc.vector.scalar_tensor_tensor(
-                out=o[:, 0:HALF], in0=ys[i][:, 0:HALF], scalar=sts[i][:, 2:3], in1=gb_v[:, 0:HALF],
+                out=o[:, 0:cv], in0=ys[i][:, 0:cv], scalar=sts[i][:, 2:3], in1=gam_ps[:, 0:cv],
                 op0=ALU.add, op1=ALU.mult,
             )
-            if cv_of(i) == E:
-                nc.vector.scalar_tensor_tensor(
-                    out=o[:, HALF:E], in0=ys[i][:, HALF:E], scalar=sts[i][:, 2:3], in1=gb_g[:, 0:HALF],
-                    op0=ALU.add, op1=ALU.mult,
-                )
 
         def t2(i):
-            o = os_[i]
+            o, cv = os_[i], cv_of(i)
             nc.vector.scalar_tensor_tensor(
-                out=o[:, 0:HALF], in0=o[:, 0:HALF], scalar=sts[i][:, 5:6], in1=gb_v[:, HALF:E],
+                out=o[:, 0:cv], in0=o[:, 0:cv], scalar=sts[i][:, 5:6], in1=bet_ps[:, 0:cv],
                 op0=ALU.mult, op1=ALU.add,
             )
-            if cv_of(i) == E:
-                nc.vector.scalar_tensor_tensor(
-                    out=o[:, HALF:E], in0=o[:, HALF:E], scalar=sts[i][:, 5:6], in1=gb_g[:, HALF:E],
-                    op0=ALU.mult, op1=ALU.add,
-                )
-
-        def zg(i):
-            if cv_of(i) == E:
-                return
-            st, o = sts[i], os_[i]
-            nc.scalar.activation(out=st[:, 6:7], in_=st[:, 2:3], func=ACT.Identity, scale=st[:, 5:6])
-            nc.scalar.activation(out=o[:, HALF:E], in_=ys[i][:, HALF:E], func=ACT.Identity,
-                                 scale=st[:, 5:6], bias=st[:, 6:7])
-            nc.gpsimd.tensor_tensor(out=o[:, HALF:E], in0=o[:, HALF:E], in1=gb_g[:, 0:HALF], op=ALU.mult)
-            nc.gpsimd.tensor_tensor(out=o[:, HALF:E], in0=o[:, HALF:E], in1=gb_g[:, HALF:E], op=ALU.add)
 
         def store(i):
             r, j = divmod(i, 2)
             nc.sync.dma_start(out=o_v[r][:, j, :], in_=os_[i][:])
 
+        gb_bcast()
         wcopy(0)
         wcopy(1)
+        gb_copy()
         wq(0)
-        wq(1)
         trp(0)
-        trp(1)
         cpo(0)
-        cpo(1)
+        wq(1)
         wcopy(2)
-        quant(0)
-        wcopy(3)
+        quant(0, 1)
         wq(2)
-        gb_bcast()
+        wcopy(3)
         mmh(0, 0)
-        mmh(1, 0)
+        trp(1)
+        cpo(1)
         wq(3)
+        add_x(0, 0)
+        quant(1, 1)
         mmh(0, 1)
-        mmh(1, 1)
         trp(2)
+        mm(1)
         trp(3)
+        add_x(0, 1)
+        negmean(0)
+        cpo(2)
+        sumsq(0)
+        new_o(0)
+        add_x(1, 0)
+        add_x(1, 1)
+        t1(0)
+        cpo(3)
+        rstd(0)
+        negmean(1)
+        nmr(0)
+        new_o(1)
+        t1(1)
+        quant(2, 2)
+        trp(4)
+        mm(2)
+        trp(5)
+        mm(3)
+        zs(0)
+        g1(0)
+        sumsq(1)
+        t2(0)
+        cpo(4)
+        rstd(1)
+        cpo(5)
 
-        for k in range(NT + 1):
+        for k in range(2, NT + 2):
             if k < NT:
                 add_x(k, 0)
-            if k >= 1:
-                recip(k - 1)
-            if k < NT:
                 add_x(k, 1)
-            if k == 1:
-                quant(1)
-            if k >= 2 and k % 2 == 0 and k + 3 < NT:
-                quant(k // 2 + 1)
-            if k >= 1:
-                zg(k - 1)
-                t2(k - 1)
-                store(k - 1)
-            if k < NT:
                 negmean(k)
-                t1(k)
+                new_o(k)
+            if k == 2:
+                trp(6)
+                cpo(6)
+                trp(7)
+                cpo(7)
+                quant(4, 2)
+            else:
+                trp(k + LOOK)
+                cpo(k + LOOK)
+            if k >= 4 and k % 2 == 0 and k + 3 < NT:
+                quant(k + 2, 2)
+            if k - 1 < NT - 1:
+                nmr(k - 1)
+            if k < NT:
                 sumsq(k)
-            if k == 0:
-                cpo(2)
-                cpo(3)
-            if k + 4 < NT:
-                trp(k + 4)
-                cpo(k + 4)
-            if k == 1:
-                mmh(2, 0)
-                mmh(2, 1)
-            if k >= 1 and k + 2 < NT:
-                mmh(k + 2, 0)
-                mmh(k + 2, 1)
+            if k - 1 < NT - 1:
+                zs(k - 1)
+            if k < NT:
+                rstd(k)
+            if k - 2 < NT - 1:
+                g2(k - 2)
+            if k - 1 < NT - 1:
+                g1(k - 1)
+            if k >= 3:
+                t2(k - 2)
+            store(k - 2)
+            if k >= 3 and k - 1 < NT:
+                t1(k - 1)
+            if k + 2 < NT:
+                mm(k + 2)

@@ -16,10 +16,22 @@ E = 1024
 NT = 16
 HALF = 512
 LN_EPS = 1e-6
-WV = 336
-LOOK = 5
-CV_MAIN = 560
+WV = 256
+LOOK = 6
+CV_MAIN = 512
 CV_LAST = (768, 1024)
+
+
+GROUPS = (1, 1, 2, 2, 2, 4, 4)
+
+
+def group_of(i):
+    first = 0
+    for n in GROUPS:
+        if i < first + n:
+            return first, n
+        first += n
+    return first, 0
 
 
 def cv_of(i):
@@ -163,18 +175,19 @@ def tile_selfattention_pa_kernel(tc, h_attn, x, out_w, ln_gamma, ln_beta, out):
         def cpo(i):
             if i >= NT:
                 return
-            if i < 2 or i % 2 == 0:
-                grp = gpool.tile([P, 2 * E], BF16, name="m_grp", tag="m_grp", align_bytes=64)
-                m_grp[i] = (grp, 0)
-                if i >= 2:
-                    m_grp[i + 1] = (grp, 1)
+            first, n = group_of(i)
+            if i == first:
+                grp = gpool.tile([P, 4 * E], BF16, name="m_grp", tag="m_grp", align_bytes=64)
+                for s in range(n):
+                    m_grp[first + s] = (grp, s)
             grp, s = m_grp[i]
             dst = grp[:, s * E:(s + 1) * E].bitcast(F32).rearrange("p (g r u) -> p g r u", g=2, u=2)
             nc.scalar.copy(out=dst, in_=xts[i][:].rearrange("p (g u r) -> p g r u", g=2, u=2))
 
-        def quant(i, n):
-            mc = mqpool.tile([P, HALF], U32, name="mc", tag="mc", align_bytes=64)
-            ms = mqpool.tile([P, HALF], U8, name="ms", tag="ms", align_bytes=64)
+        def quant(i):
+            first, n = group_of(i)
+            mc = mqpool.tile([P, 4 * 256], U32, name="mc", tag="mc", align_bytes=64)
+            ms = mqpool.tile([P, 4 * 256], U8, name="ms", tag="ms", align_bytes=64)
             grp = m_grp[i][0]
             nc.vector.quantize_mx(out=mc[:, 0:n * 256].bitcast(E5X4), scales=ms[:, 0:n * 256], in_=grp[:, 0:n * E])
             for s in range(n):
@@ -259,35 +272,35 @@ def tile_selfattention_pa_kernel(tc, h_attn, x, out_w, ln_gamma, ln_beta, out):
                 op0=ALU.add, op1=ALU.mult,
             )
 
-        def t2(i):
-            o, cv = os_[i], cv_of(i)
+        def t2(i, c0, c1):
+            o = os_[i]
             nc.vector.scalar_tensor_tensor(
-                out=o[:, 0:cv], in0=o[:, 0:cv], scalar=sts[i][:, 5:6], in1=bet_ps[:, 0:cv],
+                out=o[:, c0:c1], in0=o[:, c0:c1], scalar=sts[i][:, 5:6], in1=bet_ps[:, c0:c1],
                 op0=ALU.mult, op1=ALU.add,
             )
 
-        def store(i):
+        def store(i, c0, c1):
             r, j = divmod(i, 2)
-            nc.sync.dma_start(out=o_v[r][:, j, :], in_=os_[i][:])
+            nc.sync.dma_start(out=o_v[r][:, j, c0:c1], in_=os_[i][:, c0:c1])
 
         gb_bcast()
         wcopy(0)
         wcopy(1)
-        gb_copy()
         wq(0)
         trp(0)
         cpo(0)
         wq(1)
         wcopy(2)
-        quant(0, 1)
+        quant(0)
         wq(2)
         wcopy(3)
+        gb_copy()
         mmh(0, 0)
         trp(1)
         cpo(1)
         wq(3)
         add_x(0, 0)
-        quant(1, 1)
+        quant(1)
         mmh(0, 1)
         trp(2)
         mm(1)
@@ -306,7 +319,7 @@ def tile_selfattention_pa_kernel(tc, h_attn, x, out_w, ln_gamma, ln_beta, out):
         nmr(0)
         new_o(1)
         t1(1)
-        quant(2, 2)
+        quant(2)
         trp(4)
         mm(2)
         trp(5)
@@ -314,7 +327,7 @@ def tile_selfattention_pa_kernel(tc, h_attn, x, out_w, ln_gamma, ln_beta, out):
         zs(0)
         g1(0)
         sumsq(1)
-        t2(0)
+        t2(0, 0, cv_of(0))
         cpo(4)
         rstd(1)
         cpo(5)
@@ -325,17 +338,16 @@ def tile_selfattention_pa_kernel(tc, h_attn, x, out_w, ln_gamma, ln_beta, out):
                 add_x(k, 1)
                 negmean(k)
                 new_o(k)
-            if k == 2:
-                trp(6)
-                cpo(6)
-                trp(7)
-                cpo(7)
-                quant(4, 2)
+            if k < 4:
+                trp(2 * k + 2)
+                cpo(2 * k + 2)
+                trp(2 * k + 3)
+                cpo(2 * k + 3)
             else:
                 trp(k + LOOK)
                 cpo(k + LOOK)
-            if k >= 4 and k % 2 == 0 and k + 3 < NT:
-                quant(k + 2, 2)
+            if k + 2 < NT and group_of(k + 2)[0] == k + 2:
+                quant(k + 2)
             if k - 1 < NT - 1:
                 nmr(k - 1)
             if k < NT:
@@ -348,9 +360,15 @@ def tile_selfattention_pa_kernel(tc, h_attn, x, out_w, ln_gamma, ln_beta, out):
                 g2(k - 2)
             if k - 1 < NT - 1:
                 g1(k - 1)
-            if k >= 3:
-                t2(k - 2)
-            store(k - 2)
+            if k - 2 == NT - 1:
+                t2(k - 2, 0, HALF)
+                store(k - 2, 0, HALF)
+                t2(k - 2, HALF, E)
+                store(k - 2, HALF, E)
+            else:
+                if k >= 3:
+                    t2(k - 2, 0, cv_of(k - 2))
+                store(k - 2, 0, E)
             if k >= 3 and k - 1 < NT:
                 t1(k - 1)
             if k + 2 < NT:

@@ -16,22 +16,10 @@ E = 1024
 NT = 16
 HALF = 512
 LN_EPS = 1e-6
-WV = 256
-LOOK = 6
-CV_MAIN = 512
+WV = 336
+LOOK = 5
+CV_MAIN = 608
 CV_LAST = (768, 1024)
-
-
-GROUPS = (1, 1, 2, 2, 2, 4, 4)
-
-
-def group_of(i):
-    first = 0
-    for n in GROUPS:
-        if i < first + n:
-            return first, n
-        first += n
-    return first, 0
 
 
 def cv_of(i):
@@ -175,19 +163,18 @@ def tile_selfattention_pa_kernel(tc, h_attn, x, out_w, ln_gamma, ln_beta, out):
         def cpo(i):
             if i >= NT:
                 return
-            first, n = group_of(i)
-            if i == first:
-                grp = gpool.tile([P, 4 * E], BF16, name="m_grp", tag="m_grp", align_bytes=64)
-                for s in range(n):
-                    m_grp[first + s] = (grp, s)
+            if i < 2 or i % 2 == 0:
+                grp = gpool.tile([P, 2 * E], BF16, name="m_grp", tag="m_grp", align_bytes=64)
+                m_grp[i] = (grp, 0)
+                if i >= 2:
+                    m_grp[i + 1] = (grp, 1)
             grp, s = m_grp[i]
             dst = grp[:, s * E:(s + 1) * E].bitcast(F32).rearrange("p (g r u) -> p g r u", g=2, u=2)
             nc.scalar.copy(out=dst, in_=xts[i][:].rearrange("p (g u r) -> p g r u", g=2, u=2))
 
-        def quant(i):
-            first, n = group_of(i)
-            mc = mqpool.tile([P, 4 * 256], U32, name="mc", tag="mc", align_bytes=64)
-            ms = mqpool.tile([P, 4 * 256], U8, name="ms", tag="ms", align_bytes=64)
+        def quant(i, n):
+            mc = mqpool.tile([P, HALF], U32, name="mc", tag="mc", align_bytes=64)
+            ms = mqpool.tile([P, HALF], U8, name="ms", tag="ms", align_bytes=64)
             grp = m_grp[i][0]
             nc.vector.quantize_mx(out=mc[:, 0:n * 256].bitcast(E5X4), scales=ms[:, 0:n * 256], in_=grp[:, 0:n * E])
             for s in range(n):
@@ -272,35 +259,35 @@ def tile_selfattention_pa_kernel(tc, h_attn, x, out_w, ln_gamma, ln_beta, out):
                 op0=ALU.add, op1=ALU.mult,
             )
 
-        def t2(i, c0, c1):
-            o = os_[i]
+        def t2(i):
+            o, cv = os_[i], cv_of(i)
             nc.vector.scalar_tensor_tensor(
-                out=o[:, c0:c1], in0=o[:, c0:c1], scalar=sts[i][:, 5:6], in1=bet_ps[:, c0:c1],
+                out=o[:, 0:cv], in0=o[:, 0:cv], scalar=sts[i][:, 5:6], in1=bet_ps[:, 0:cv],
                 op0=ALU.mult, op1=ALU.add,
             )
 
-        def store(i, c0, c1):
+        def store(i):
             r, j = divmod(i, 2)
-            nc.sync.dma_start(out=o_v[r][:, j, c0:c1], in_=os_[i][:, c0:c1])
+            nc.sync.dma_start(out=o_v[r][:, j, :], in_=os_[i][:])
 
         gb_bcast()
         wcopy(0)
         wcopy(1)
+        gb_copy()
         wq(0)
         trp(0)
         cpo(0)
         wq(1)
         wcopy(2)
-        quant(0)
+        quant(0, 1)
         wq(2)
         wcopy(3)
-        gb_copy()
         mmh(0, 0)
         trp(1)
         cpo(1)
         wq(3)
         add_x(0, 0)
-        quant(1)
+        quant(1, 1)
         mmh(0, 1)
         trp(2)
         mm(1)
@@ -319,7 +306,7 @@ def tile_selfattention_pa_kernel(tc, h_attn, x, out_w, ln_gamma, ln_beta, out):
         nmr(0)
         new_o(1)
         t1(1)
-        quant(2)
+        quant(2, 2)
         trp(4)
         mm(2)
         trp(5)
@@ -327,7 +314,7 @@ def tile_selfattention_pa_kernel(tc, h_attn, x, out_w, ln_gamma, ln_beta, out):
         zs(0)
         g1(0)
         sumsq(1)
-        t2(0, 0, cv_of(0))
+        t2(0)
         cpo(4)
         rstd(1)
         cpo(5)
@@ -338,16 +325,17 @@ def tile_selfattention_pa_kernel(tc, h_attn, x, out_w, ln_gamma, ln_beta, out):
                 add_x(k, 1)
                 negmean(k)
                 new_o(k)
-            if k < 4:
-                trp(2 * k + 2)
-                cpo(2 * k + 2)
-                trp(2 * k + 3)
-                cpo(2 * k + 3)
+            if k == 2:
+                trp(6)
+                cpo(6)
+                trp(7)
+                cpo(7)
+                quant(4, 2)
             else:
                 trp(k + LOOK)
                 cpo(k + LOOK)
-            if k + 2 < NT and group_of(k + 2)[0] == k + 2:
-                quant(k + 2)
+            if k >= 4 and k % 2 == 0 and k + 3 < NT:
+                quant(k + 2, 2)
             if k - 1 < NT - 1:
                 nmr(k - 1)
             if k < NT:
@@ -360,15 +348,9 @@ def tile_selfattention_pa_kernel(tc, h_attn, x, out_w, ln_gamma, ln_beta, out):
                 g2(k - 2)
             if k - 1 < NT - 1:
                 g1(k - 1)
-            if k - 2 == NT - 1:
-                t2(k - 2, 0, HALF)
-                store(k - 2, 0, HALF)
-                t2(k - 2, HALF, E)
-                store(k - 2, HALF, E)
-            else:
-                if k >= 3:
-                    t2(k - 2, 0, cv_of(k - 2))
-                store(k - 2, 0, E)
+            if k >= 3:
+                t2(k - 2)
+            store(k - 2)
             if k >= 3 and k - 1 < NT:
                 t1(k - 1)
             if k + 2 < NT:

@@ -17,9 +17,21 @@ NT = 16
 HALF = 512
 LN_EPS = 1e-6
 WV = 336
-LOOK = 5
-CV_MAIN = 608
+LOOK = 6
+CV_MAIN = 584
 CV_LAST = (768, 1024)
+
+
+GROUPS = (1, 1, 2, 2, 2, 4, 4)
+
+
+def group_of(i):
+    first = 0
+    for n in GROUPS:
+        if i < first + n:
+            return first, n
+        first += n
+    return first, 0
 
 
 def cv_of(i):
@@ -160,21 +172,26 @@ def tile_selfattention_pa_kernel(tc, h_attn, x, out_w, ln_gamma, ln_beta, out):
                     )
             xts[i] = xt
 
-        def cpo(i):
+        def cpo(i, on_vector=False):
             if i >= NT:
                 return
-            if i < 2 or i % 2 == 0:
-                grp = gpool.tile([P, 2 * E], BF16, name="m_grp", tag="m_grp", align_bytes=64)
-                m_grp[i] = (grp, 0)
-                if i >= 2:
-                    m_grp[i + 1] = (grp, 1)
+            first, n = group_of(i)
+            if i == first:
+                grp = gpool.tile([P, 4 * E], BF16, name="m_grp", tag="m_grp", align_bytes=64)
+                for s in range(n):
+                    m_grp[first + s] = (grp, s)
             grp, s = m_grp[i]
             dst = grp[:, s * E:(s + 1) * E].bitcast(F32).rearrange("p (g r u) -> p g r u", g=2, u=2)
-            nc.scalar.copy(out=dst, in_=xts[i][:].rearrange("p (g u r) -> p g r u", g=2, u=2))
+            src = xts[i][:].rearrange("p (g u r) -> p g r u", g=2, u=2)
+            if on_vector:
+                nc.vector.tensor_copy(out=dst, in_=src)
+            else:
+                nc.scalar.copy(out=dst, in_=src)
 
-        def quant(i, n):
-            mc = mqpool.tile([P, HALF], U32, name="mc", tag="mc", align_bytes=64)
-            ms = mqpool.tile([P, HALF], U8, name="ms", tag="ms", align_bytes=64)
+        def quant(i):
+            first, n = group_of(i)
+            mc = mqpool.tile([P, 4 * 256], U32, name="mc", tag="mc", align_bytes=64)
+            ms = mqpool.tile([P, 4 * 256], U8, name="ms", tag="ms", align_bytes=64)
             grp = m_grp[i][0]
             nc.vector.quantize_mx(out=mc[:, 0:n * 256].bitcast(E5X4), scales=ms[:, 0:n * 256], in_=grp[:, 0:n * E])
             for s in range(n):
@@ -259,16 +276,16 @@ def tile_selfattention_pa_kernel(tc, h_attn, x, out_w, ln_gamma, ln_beta, out):
                 op0=ALU.add, op1=ALU.mult,
             )
 
-        def t2(i):
-            o, cv = os_[i], cv_of(i)
+        def t2(i, c0, c1):
+            o = os_[i]
             nc.vector.scalar_tensor_tensor(
-                out=o[:, 0:cv], in0=o[:, 0:cv], scalar=sts[i][:, 5:6], in1=bet_ps[:, 0:cv],
+                out=o[:, c0:c1], in0=o[:, c0:c1], scalar=sts[i][:, 5:6], in1=bet_ps[:, c0:c1],
                 op0=ALU.mult, op1=ALU.add,
             )
 
-        def store(i):
+        def store(i, c0, c1):
             r, j = divmod(i, 2)
-            nc.sync.dma_start(out=o_v[r][:, j, :], in_=os_[i][:])
+            nc.sync.dma_start(out=o_v[r][:, j, c0:c1], in_=os_[i][:, c0:c1])
 
         gb_bcast()
         wcopy(0)
@@ -279,7 +296,7 @@ def tile_selfattention_pa_kernel(tc, h_attn, x, out_w, ln_gamma, ln_beta, out):
         cpo(0)
         wq(1)
         wcopy(2)
-        quant(0, 1)
+        quant(0)
         wq(2)
         wcopy(3)
         mmh(0, 0)
@@ -287,34 +304,34 @@ def tile_selfattention_pa_kernel(tc, h_attn, x, out_w, ln_gamma, ln_beta, out):
         cpo(1)
         wq(3)
         add_x(0, 0)
-        quant(1, 1)
+        quant(1)
         mmh(0, 1)
         trp(2)
         mm(1)
         trp(3)
         add_x(0, 1)
         negmean(0)
-        cpo(2)
+        cpo(2, on_vector=True)
         sumsq(0)
         new_o(0)
         add_x(1, 0)
         add_x(1, 1)
+        cpo(3, on_vector=True)
         t1(0)
-        cpo(3)
-        rstd(0)
-        negmean(1)
-        nmr(0)
-        new_o(1)
-        t1(1)
-        quant(2, 2)
+        quant(2)
         trp(4)
         mm(2)
         trp(5)
         mm(3)
+        rstd(0)
+        nmr(0)
         zs(0)
         g1(0)
+        negmean(1)
+        new_o(1)
+        t1(1)
+        t2(0, 0, cv_of(0))
         sumsq(1)
-        t2(0)
         cpo(4)
         rstd(1)
         cpo(5)
@@ -325,17 +342,16 @@ def tile_selfattention_pa_kernel(tc, h_attn, x, out_w, ln_gamma, ln_beta, out):
                 add_x(k, 1)
                 negmean(k)
                 new_o(k)
-            if k == 2:
-                trp(6)
-                cpo(6)
-                trp(7)
-                cpo(7)
-                quant(4, 2)
+            if k < 4:
+                trp(2 * k + 2)
+                cpo(2 * k + 2)
+                trp(2 * k + 3)
+                cpo(2 * k + 3)
             else:
                 trp(k + LOOK)
                 cpo(k + LOOK)
-            if k >= 4 and k % 2 == 0 and k + 3 < NT:
-                quant(k + 2, 2)
+            if k + 2 < NT and group_of(k + 2)[0] == k + 2:
+                quant(k + 2)
             if k - 1 < NT - 1:
                 nmr(k - 1)
             if k < NT:
@@ -348,9 +364,15 @@ def tile_selfattention_pa_kernel(tc, h_attn, x, out_w, ln_gamma, ln_beta, out):
                 g2(k - 2)
             if k - 1 < NT - 1:
                 g1(k - 1)
-            if k >= 3:
-                t2(k - 2)
-            store(k - 2)
+            if k - 2 == NT - 1:
+                t2(k - 2, 0, HALF)
+                store(k - 2, 0, HALF)
+                t2(k - 2, HALF, E)
+                store(k - 2, HALF, E)
+            else:
+                if k >= 3:
+                    t2(k - 2, 0, cv_of(k - 2))
+                store(k - 2, 0, E)
             if k >= 3 and k - 1 < NT:
                 t1(k - 1)
             if k + 2 < NT:

@@ -16,7 +16,7 @@ E = 1024
 NT = 16
 HALF = 512
 LN_EPS = 1e-6
-WV = 336
+WV = 320
 LOOK = 6
 CV_MAIN = 584
 CV_LAST = (768, 1024)
@@ -52,7 +52,7 @@ def tile_selfattention_pa_kernel(tc, h_attn, x, out_w, ln_gamma, ln_beta, out):
         const = ctx.enter_context(tc.tile_pool(name="const", bufs=1))
         hpool = ctx.enter_context(tc.tile_pool(name="hpool", bufs=NT))
         xpool = ctx.enter_context(tc.tile_pool(name="xpool", bufs=NT // 2))
-        wrpool = ctx.enter_context(tc.tile_pool(name="wrpool", bufs=4))
+        wrpool = ctx.enter_context(tc.tile_pool(name="wrpool", bufs=5))
         wgpool = ctx.enter_context(tc.tile_pool(name="wgpool", bufs=2))
         gpool = ctx.enter_context(tc.tile_pool(name="gpool", bufs=3))
         mqpool = ctx.enter_context(tc.tile_pool(name="mqpool", bufs=4))
@@ -68,11 +68,14 @@ def tile_selfattention_pa_kernel(tc, h_attn, x, out_w, ln_gamma, ln_beta, out):
         hs = {}
         xs = {}
 
-        def load_w(c):
+        def load_w(c, pieces=1):
             half, g = divmod(c, 2)
-            t = wrpool.tile([P, 4, HALF], BF16, name="w_raw", tag="w_raw")
-            nc.sync.dma_start(out=t[:], in_=w_v[g][:, :, half * HALF:(half + 1) * HALF])
-            w_raw[c] = t
+            width = HALF // pieces
+            w_raw[c] = []
+            for s in range(pieces):
+                t = wrpool.tile([P, 4, width], BF16, name="w_raw", tag="w_raw")
+                nc.sync.dma_start(out=t[:], in_=w_v[g][:, :, half * HALF + s * width:half * HALF + (s + 1) * width])
+                w_raw[c].append(t)
 
         def load_h(i):
             r, j = divmod(i, 2)
@@ -84,13 +87,16 @@ def tile_selfattention_pa_kernel(tc, h_attn, x, out_w, ln_gamma, ln_beta, out):
         def new_x(r):
             xs[r] = xpool.tile([P, 2, E], BF16, name="xs", tag="xs")
 
-        gb_stage = const.tile([1, 2 * E], BF16, name="gb_stage")
-        nc.sync.dma_start(out=gb_stage[0:1, 0:E], in_=ln_gamma.rearrange("(o e) -> o e", o=1))
-        nc.sync.dma_start(out=gb_stage[0:1, E:2 * E], in_=ln_beta.rearrange("(o e) -> o e", o=1))
-        load_w(0)
+        ident = const.tile([P, P], F32, name="ident")
+        make_identity(nc, ident[:])
+        gb_row = const.tile([P, 2 * E], BF16, name="gb_row")
+        nc.vector.memset(gb_row[:], 0.0)
+        load_w(0, pieces=2)
         load_w(1)
-        load_h(0)
         load_w(2)
+        load_h(0)
+        nc.sync.dma_start(out=gb_row[0:1, 0:E], in_=ln_gamma.rearrange("(o e) -> o e", o=1))
+        nc.sync.dma_start(out=gb_row[0:1, E:2 * E], in_=ln_beta.rearrange("(o e) -> o e", o=1))
         load_w(3)
         new_x(0)
         nc.sync.dma_start(out=xs[0][:, 0, :], in_=x_v[0][:, 0, :])
@@ -102,17 +108,12 @@ def tile_selfattention_pa_kernel(tc, h_attn, x, out_w, ln_gamma, ln_beta, out):
             new_x(r)
             nc.sync.dma_start(out=xs[r][:], in_=x_v[r])
 
-        gb_row = const.tile([P, 2 * E], BF16, name="gb_row")
-        nc.vector.memset(gb_row[:], 0.0)
         ones = const.tile([P, P], BF16, name="ones")
         nc.vector.memset(ones[:], 1.0)
         warm = const.tile([P, 1], F32, name="warm")
         nc.vector.memset(warm[:], 1.0)
-        ident = const.tile([P, P], F32, name="ident")
-        make_identity(nc, ident[:])
         warm2 = const.tile([P, 1], F32, name="warm2")
         nc.scalar.activation(out=warm2[:], in_=warm[:], func=ACT.Abs_reciprocal_sqrt)
-        nc.scalar.copy(out=gb_row[0:1, :], in_=gb_stage[0:1, :])
 
         gam_ps = ps_gb.tile([P, E], BF16, name="gam_ps")
         bet_ps = ps_gb.tile([P, E], BF16, name="bet_ps")
@@ -132,17 +133,27 @@ def tile_selfattention_pa_kernel(tc, h_attn, x, out_w, ln_gamma, ln_beta, out):
                 nc.tensor.matmul(out=bet_ps[:, cols], lhsT=ones[:], rhs=gb_row[:, E + half * HALF:E + (half + 1) * HALF],
                                  start=True, stop=True)
 
+        def warm_pe(c):
+            for t in w_raw[c]:
+                width = t.shape[2]
+                for row in range(2):
+                    nc.tensor.matmul(out=gam_ps[:, 0:width], lhsT=ones[:], rhs=t[:, row, :], start=True, stop=True)
+
         def gb_copy():
             nc.scalar.copy(out=gam_sb[:, CV_MAIN:E], in_=gam_ps[:, CV_MAIN:E])
             nc.scalar.copy(out=bet_sb[:, CV_MAIN:E], in_=bet_ps[:, CV_MAIN:E])
 
         w_grp = {}
 
-        def wcopy(c):
+        def wcopy(c, pieces=1):
             grp = wgpool.tile([P, HALF, 4], BF16, name="w_grp", tag="w_grp", align_bytes=64)
-            src = w_raw[c][:].rearrange("p t n -> p n t")
-            nc.vector.tensor_copy(out=grp[:, 0:WV, :], in_=src[:, 0:WV, :])
-            nc.scalar.copy(out=grp[:, WV:HALF, :], in_=src[:, WV:HALF, :])
+            width = HALF // pieces
+            wv = WV // pieces
+            for s in range(pieces):
+                src = w_raw[c][s][:].rearrange("p t n -> p n t")
+                c0 = s * width
+                nc.vector.tensor_copy(out=grp[:, c0:c0 + wv, :], in_=src[:, 0:wv, :])
+                nc.scalar.copy(out=grp[:, c0 + wv:c0 + width, :], in_=src[:, wv:width, :])
             w_grp[c] = grp
 
         def wq(c):
@@ -287,20 +298,23 @@ def tile_selfattention_pa_kernel(tc, h_attn, x, out_w, ln_gamma, ln_beta, out):
             r, j = divmod(i, 2)
             nc.sync.dma_start(out=o_v[r][:, j, c0:c1], in_=os_[i][:, c0:c1])
 
-        gb_bcast()
-        wcopy(0)
-        wcopy(1)
-        gb_copy()
+        warm_pe(0)
+        wcopy(0, pieces=2)
         wq(0)
-        trp(0)
-        cpo(0)
+        warm_pe(1)
+        wcopy(1)
         wq(1)
+        warm_pe(2)
         wcopy(2)
-        quant(0)
+        trp(0)
+        gb_bcast()
+        cpo(0)
         wq(2)
         wcopy(3)
-        mmh(0, 0)
+        quant(0)
+        gb_copy()
         trp(1)
+        mmh(0, 0)
         cpo(1)
         wq(3)
         add_x(0, 0)

@@ -91,12 +91,13 @@ def tile_selfattention_pa_kernel(tc, h_attn, x, out_w, ln_gamma, ln_beta, out):
         make_identity(nc, ident[:])
         gb_row = const.tile([P, 2 * E], BF16, name="gb_row")
         nc.vector.memset(gb_row[:], 0.0)
+        gb_stage = const.tile([1, 2 * E], BF16, name="gb_stage")
+        nc.sync.dma_start(out=gb_stage[0:1, 0:E], in_=ln_gamma.rearrange("(o e) -> o e", o=1))
+        nc.sync.dma_start(out=gb_stage[0:1, E:2 * E], in_=ln_beta.rearrange("(o e) -> o e", o=1))
         load_w(0, pieces=2)
         load_w(1)
         load_w(2)
         load_h(0)
-        nc.sync.dma_start(out=gb_row[0:1, 0:E], in_=ln_gamma.rearrange("(o e) -> o e", o=1))
-        nc.sync.dma_start(out=gb_row[0:1, E:2 * E], in_=ln_beta.rearrange("(o e) -> o e", o=1))
         load_w(3)
         new_x(0)
         nc.sync.dma_start(out=xs[0][:, 0, :], in_=x_v[0][:, 0, :])
@@ -112,6 +113,7 @@ def tile_selfattention_pa_kernel(tc, h_attn, x, out_w, ln_gamma, ln_beta, out):
         nc.vector.memset(ones[:], 1.0)
         warm = const.tile([P, 1], F32, name="warm")
         nc.vector.memset(warm[:], 1.0)
+        nc.vector.tensor_copy(out=gb_row[0:1, :], in_=gb_stage[0:1, :])
         warm2 = const.tile([P, 1], F32, name="warm2")
         nc.scalar.activation(out=warm2[:], in_=warm[:], func=ACT.Abs_reciprocal_sqrt)
 

@@ -16,7 +16,7 @@ E = 1024
 NT = 16
 HALF = 512
 LN_EPS = 1e-6
-WV = 320
+WV = 288
 LOOK = 6
 CV_MAIN = 584
 CV_LAST = (768, 1024)
@@ -53,7 +53,7 @@ def tile_selfattention_pa_kernel(tc, h_attn, x, out_w, ln_gamma, ln_beta, out):
         hpool = ctx.enter_context(tc.tile_pool(name="hpool", bufs=NT))
         xpool = ctx.enter_context(tc.tile_pool(name="xpool", bufs=NT // 2))
         wrpool = ctx.enter_context(tc.tile_pool(name="wrpool", bufs=5))
-        wgpool = ctx.enter_context(tc.tile_pool(name="wgpool", bufs=2))
+        wgpool = ctx.enter_context(tc.tile_pool(name="wgpool", bufs=4))
         gpool = ctx.enter_context(tc.tile_pool(name="gpool", bufs=3))
         mqpool = ctx.enter_context(tc.tile_pool(name="mqpool", bufs=4))
         ypool = ctx.enter_context(tc.tile_pool(name="ypool", bufs=5))
@@ -158,14 +158,16 @@ def tile_selfattention_pa_kernel(tc, h_attn, x, out_w, ln_gamma, ln_beta, out):
                 nc.scalar.copy(out=grp[:, c0 + wv:c0 + width, :], in_=src[:, wv:width, :])
             w_grp[c] = grp
 
-        def wq(c):
+        def wq(c, pieces=1):
             half, g = divmod(c, 2)
-            cols = slice(half * HALF, (half + 1) * HALF)
-            nc.vector.quantize_mx(
-                out=w_codes[:, g, cols].bitcast(E5X4),
-                scales=w_scales[:, g, cols],
-                in_=w_grp[c][:].rearrange("p n t -> p (n t)"),
-            )
+            width = HALF // pieces
+            for s in range(pieces):
+                cols = slice(half * HALF + s * width, half * HALF + (s + 1) * width)
+                nc.vector.quantize_mx(
+                    out=w_codes[:, g, cols].bitcast(E5X4),
+                    scales=w_scales[:, g, cols],
+                    in_=w_grp[c][:, s * width:(s + 1) * width, :].rearrange("p n t -> p (n t)"),
+                )
 
         m_grp = {}
         m_q = {}
@@ -302,22 +304,22 @@ def tile_selfattention_pa_kernel(tc, h_attn, x, out_w, ln_gamma, ln_beta, out):
 
         warm_pe(0)
         wcopy(0, pieces=2)
-        wq(0)
+        wq(0, pieces=2)
         warm_pe(1)
         wcopy(1)
-        wq(1)
         warm_pe(2)
         wcopy(2)
+        wq(1)
         trp(0)
         gb_bcast()
         cpo(0)
-        wq(2)
         wcopy(3)
         quant(0)
-        gb_copy()
+        wq(2)
         trp(1)
         mmh(0, 0)
         cpo(1)
+        gb_copy()
         wq(3)
         add_x(0, 0)
         quant(1)
@@ -325,14 +327,14 @@ def tile_selfattention_pa_kernel(tc, h_attn, x, out_w, ln_gamma, ln_beta, out):
         trp(2)
         mm(1)
         trp(3)
+        cpo(2)
         add_x(0, 1)
         negmean(0)
-        cpo(2, on_vector=True)
         sumsq(0)
+        cpo(3)
         new_o(0)
         add_x(1, 0)
         add_x(1, 1)
-        cpo(3, on_vector=True)
         t1(0)
         quant(2)
         trp(4)

@@ -52,7 +52,7 @@ def tile_selfattention_pa_kernel(tc, h_attn, x, out_w, ln_gamma, ln_beta, out):
         const = ctx.enter_context(tc.tile_pool(name="const", bufs=1))
         hpool = ctx.enter_context(tc.tile_pool(name="hpool", bufs=NT))
         xpool = ctx.enter_context(tc.tile_pool(name="xpool", bufs=NT // 2))
-        wrpool = ctx.enter_context(tc.tile_pool(name="wrpool", bufs=5))
+        wrpool = ctx.enter_context(tc.tile_pool(name="wrpool", bufs=2))
         wgpool = ctx.enter_context(tc.tile_pool(name="wgpool", bufs=4))
         gpool = ctx.enter_context(tc.tile_pool(name="gpool", bufs=3))
         mqpool = ctx.enter_context(tc.tile_pool(name="mqpool", bufs=4))
@@ -68,14 +68,10 @@ def tile_selfattention_pa_kernel(tc, h_attn, x, out_w, ln_gamma, ln_beta, out):
         hs = {}
         xs = {}
 
-        def load_w(c, pieces=1):
-            half, g = divmod(c, 2)
-            width = HALF // pieces
-            w_raw[c] = []
-            for s in range(pieces):
-                t = wrpool.tile([P, 4, width], BF16, name="w_raw", tag="w_raw")
-                nc.sync.dma_start(out=t[:], in_=w_v[g][:, :, half * HALF + s * width:half * HALF + (s + 1) * width])
-                w_raw[c].append(t)
+        def load_w(g):
+            t = wrpool.tile([P, 4, E], BF16, name="w_raw", tag="w_raw")
+            nc.sync.dma_start(out=t[:], in_=w_v[g])
+            w_raw[g] = t
 
         def load_h(i):
             r, j = divmod(i, 2)
@@ -94,11 +90,9 @@ def tile_selfattention_pa_kernel(tc, h_attn, x, out_w, ln_gamma, ln_beta, out):
         gb_stage = const.tile([1, 2 * E], BF16, name="gb_stage")
         nc.sync.dma_start(out=gb_stage[0:1, 0:E], in_=ln_gamma.rearrange("(o e) -> o e", o=1))
         nc.sync.dma_start(out=gb_stage[0:1, E:2 * E], in_=ln_beta.rearrange("(o e) -> o e", o=1))
-        load_w(0, pieces=2)
+        load_w(0)
         load_w(1)
-        load_w(2)
         load_h(0)
-        load_w(3)
         new_x(0)
         nc.sync.dma_start(out=xs[0][:, 0, :], in_=x_v[0][:, 0, :])
         load_h(1)
@@ -135,11 +129,9 @@ def tile_selfattention_pa_kernel(tc, h_attn, x, out_w, ln_gamma, ln_beta, out):
                 nc.tensor.matmul(out=bet_ps[:, cols], lhsT=ones[:], rhs=gb_row[:, E + half * HALF:E + (half + 1) * HALF],
                                  start=True, stop=True)
 
-        def warm_pe(c):
-            for t in w_raw[c]:
-                width = t.shape[2]
-                for row in range(2):
-                    nc.tensor.matmul(out=gam_ps[:, 0:width], lhsT=ones[:], rhs=t[:, row, :], start=True, stop=True)
+        def warm_pe(g):
+            for row in range(4):
+                nc.tensor.matmul(out=gam_ps[:, 0:HALF], lhsT=ones[:], rhs=w_raw[g][:, row, 0:HALF], start=True, stop=True)
 
         def gb_copy():
             nc.scalar.copy(out=gam_sb[:, CV_MAIN:E], in_=gam_ps[:, CV_MAIN:E])
@@ -147,15 +139,12 @@ def tile_selfattention_pa_kernel(tc, h_attn, x, out_w, ln_gamma, ln_beta, out):
 
         w_grp = {}
 
-        def wcopy(c, pieces=1):
+        def wcopy(c):
+            half, g = divmod(c, 2)
             grp = wgpool.tile([P, HALF, 4], BF16, name="w_grp", tag="w_grp", align_bytes=64)
-            width = HALF // pieces
-            wv = WV // pieces
-            for s in range(pieces):
-                src = w_raw[c][s][:].rearrange("p t n -> p n t")
-                c0 = s * width
-                nc.vector.tensor_copy(out=grp[:, c0:c0 + wv, :], in_=src[:, 0:wv, :])
-                nc.scalar.copy(out=grp[:, c0 + wv:c0 + width, :], in_=src[:, wv:width, :])
+            src = w_raw[g][:, :, half * HALF:(half + 1) * HALF].rearrange("p t n -> p n t")
+            nc.vector.tensor_copy(out=grp[:, 0:WV, :], in_=src[:, 0:WV, :])
+            nc.scalar.copy(out=grp[:, WV:HALF, :], in_=src[:, WV:HALF, :])
             w_grp[c] = grp
 
         def wq(c, pieces=1):
@@ -303,19 +292,18 @@ def tile_selfattention_pa_kernel(tc, h_attn, x, out_w, ln_gamma, ln_beta, out):
             nc.sync.dma_start(out=o_v[r][:, j, c0:c1], in_=os_[i][:, c0:c1])
 
         warm_pe(0)
-        wcopy(0, pieces=2)
-        wq(0, pieces=2)
+        wcopy(0)
+        wcopy(2)
+        wq(0)
+        wq(2)
         warm_pe(1)
         wcopy(1)
-        warm_pe(2)
-        wcopy(2)
+        wcopy(3)
         wq(1)
         trp(0)
         gb_bcast()
         cpo(0)
-        wcopy(3)
         quant(0)
-        wq(2)
         trp(1)
         mmh(0, 0)
         cpo(1)

@@ -83,6 +83,10 @@ def tile_selfattention_pa_kernel(tc, h_attn, x, out_w, ln_gamma, ln_beta, out):
         def new_x(r):
             xs[r] = xpool.tile([P, 2, E], BF16, name="xs", tag="xs")
 
+        def load_x(r):
+            new_x(r)
+            nc.sync.dma_start(out=xs[r][:], in_=x_v[r])
+
         ident = const.tile([P, P], F32, name="ident")
         make_identity(nc, ident[:])
         gb_row = const.tile([P, 2 * E], BF16, name="gb_row")
@@ -100,8 +104,12 @@ def tile_selfattention_pa_kernel(tc, h_attn, x, out_w, ln_gamma, ln_beta, out):
         for r in range(1, NT // 2):
             load_h(2 * r)
             load_h(2 * r + 1)
-            new_x(r)
-            nc.sync.dma_start(out=xs[r][:], in_=x_v[r])
+            if r == 2:
+                load_x(1)
+            elif r > 3:
+                load_x(r - 2)
+        load_x(NT // 2 - 2)
+        load_x(NT // 2 - 1)
 
         ones = const.tile([P, P], BF16, name="ones")
         nc.vector.memset(ones[:], 1.0)

@@ -17,12 +17,12 @@ NT = 16
 HALF = 512
 LN_EPS = 1e-6
 WV = 288
-LOOK = 6
+LOOK = 4
 CV_MAIN = 584
 CV_LAST = (768, 1024)
 
 
-GROUPS = (1, 1, 2, 2, 2, 4, 4)
+GROUPS = (1, 1, 2, 2, 2, 2, 2, 2, 2)
 
 
 def group_of(i):
@@ -356,27 +356,21 @@ def tile_selfattention_pa_kernel(tc, h_attn, x, out_w, ln_gamma, ln_beta, out):
                 add_x(k, 1)
                 negmean(k)
                 new_o(k)
-            if k < 4:
-                trp(2 * k + 2)
-                cpo(2 * k + 2)
-                trp(2 * k + 3)
-                cpo(2 * k + 3)
-            else:
-                trp(k + LOOK)
-                cpo(k + LOOK)
+            trp(k + LOOK)
+            cpo(k + LOOK)
             if k + 2 < NT and group_of(k + 2)[0] == k + 2:
                 quant(k + 2)
-            if k - 1 < NT - 1:
+            if k - 1 < NT and cv_of(k - 1) < E:
                 nmr(k - 1)
             if k < NT:
                 sumsq(k)
-            if k - 1 < NT - 1:
+            if k - 1 < NT and cv_of(k - 1) < E:
                 zs(k - 1)
             if k < NT:
                 rstd(k)
-            if k - 2 < NT - 1:
+            if k - 2 < NT and cv_of(k - 2) < E:
                 g2(k - 2)
-            if k - 1 < NT - 1:
+            if k - 1 < NT and cv_of(k - 1) < E:
                 g1(k - 1)
             if k - 2 == NT - 1:
                 t2(k - 2, 0, HALF)
@@ -384,10 +378,12 @@ def tile_selfattention_pa_kernel(tc, h_attn, x, out_w, ln_gamma, ln_beta, out):
                 t2(k - 2, HALF, E)
                 store(k - 2, HALF, E)
             else:
+                if k - 1 == NT - 1:
+                    t1(k - 1)
                 if k >= 3:
                     t2(k - 2, 0, cv_of(k - 2))
                 store(k - 2, 0, E)
-            if k >= 3 and k - 1 < NT:
+            if k >= 3 and k - 1 < NT - 1:
                 t1(k - 1)
             if k + 2 < NT:
                 mm(k + 2)

@@ -18,8 +18,8 @@ HALF = 512
 LN_EPS = 1e-6
 WV = 288
 LOOK = 4
-CV_MAIN = 584
-CV_LAST = (768, 1024)
+CV_MAIN = 568
+CV_LAST = (1024, 1024)
 
 
 GROUPS = (1, 1, 2, 2, 2, 2, 2, 2, 2)

@@ -18,8 +18,8 @@ HALF = 512
 LN_EPS = 1e-6
 WV = 288
 LOOK = 4
-CV_MAIN = 568
-CV_LAST = (1024, 1024)
+CV_MAIN = 552
+CV_LAST = (768, 1024, 1024)
 
 
 GROUPS = (1, 1, 2, 2, 2, 2, 2, 2, 2)
@@ -35,7 +35,8 @@ def group_of(i):
 
 
 def cv_of(i):
-    return CV_MAIN if i < NT - 2 else CV_LAST[i - (NT - 2)]
+    first = NT - len(CV_LAST)
+    return CV_MAIN if i < first else CV_LAST[i - first]
 
 FLOPS = 2 * 2048 * 1024 * 1024
 

from contextlib import ExitStack

import concourse.mybir as mybir
from concourse.masks import make_identity

F32 = mybir.dt.float32
BF16 = mybir.dt.bfloat16
U32 = mybir.dt.uint32
U8 = mybir.dt.uint8
E5X4 = mybir.dt.float8_e5m2_x4
ALU = mybir.AluOpType
ACT = mybir.ActivationFunctionType

P = 128
E = 1024
NT = 16
HALF = 512
LN_EPS = 1e-6
WV = 288
LOOK = 4
CV_MAIN = 552
CV_LAST = (768, 1024, 1024)


GROUPS = (1, 1, 2, 2, 2, 2, 2, 2, 2)


def group_of(i):
    first = 0
    for n in GROUPS:
        if i < first + n:
            return first, n
        first += n
    return first, 0


def cv_of(i):
    first = NT - len(CV_LAST)
    return CV_MAIN if i < first else CV_LAST[i - first]

FLOPS = 2 * 2048 * 1024 * 1024


def tile_selfattention_pa_kernel(tc, h_attn, x, out_w, ln_gamma, ln_beta, out):
    nc = tc.nc

    x_v = x.flatten_outer_dims().rearrange("(r p j) e -> r p j e", p=P, j=2)
    o_v = out.flatten_outer_dims().rearrange("(r p j) e -> r p j e", p=P, j=2)
    h_v = h_attn.rearrange("b h (q p j) d -> b q j p h d", p=P, j=2)
    w_v = out_w.rearrange("(g p t) n -> g p t n", p=P, t=4)

    with ExitStack() as ctx:
        const = ctx.enter_context(tc.tile_pool(name="const", bufs=1))
        hpool = ctx.enter_context(tc.tile_pool(name="hpool", bufs=NT))
        xpool = ctx.enter_context(tc.tile_pool(name="xpool", bufs=NT // 2))
        wrpool = ctx.enter_context(tc.tile_pool(name="wrpool", bufs=2))
        wgpool = ctx.enter_context(tc.tile_pool(name="wgpool", bufs=4))
        gpool = ctx.enter_context(tc.tile_pool(name="gpool", bufs=3))
        mqpool = ctx.enter_context(tc.tile_pool(name="mqpool", bufs=4))
        ypool = ctx.enter_context(tc.tile_pool(name="ypool", bufs=5))
        opool = ctx.enter_context(tc.tile_pool(name="opool", bufs=9))
        spool = ctx.enter_context(tc.tile_pool(name="spool", bufs=8))
        ps_gb = ctx.enter_context(tc.psum_pool(name="ps_gb", bufs=1))
        ps_acc = ctx.enter_context(tc.psum_pool(name="ps_acc", bufs=4))
        ps_t = ctx.enter_context(tc.psum_pool(name="ps_t", bufs=2))
        ctx.enter_context(tc.manual_schedule())

        w_raw = {}
        hs = {}
        xs = {}

        def load_w(g):
            t = wrpool.tile([P, 4, E], BF16, name="w_raw", tag="w_raw")
            nc.sync.dma_start(out=t[:], in_=w_v[g])
            w_raw[g] = t

        def load_h(i):
            r, j = divmod(i, 2)
            b, q = divmod(r, 4)
            t = hpool.tile([P, E], BF16, name="hs", tag="hs")
            nc.sync.dma_start(out=t[:].rearrange("p (h d) -> p h d", h=4), in_=h_v[b, q, j])
            hs[i] = t

        def new_x(r):
            xs[r] = xpool.tile([P, 2, E], BF16, name="xs", tag="xs")

        def load_x(r):
            new_x(r)
            nc.sync.dma_start(out=xs[r][:], in_=x_v[r])

        ident = const.tile([P, P], F32, name="ident")
        make_identity(nc, ident[:])
        gb_row = const.tile([P, 2 * E], BF16, name="gb_row")
        nc.vector.memset(gb_row[:], 0.0)
        gb_stage = const.tile([1, 2 * E], BF16, name="gb_stage")
        nc.sync.dma_start(out=gb_stage[0:1, 0:E], in_=ln_gamma.rearrange("(o e) -> o e", o=1))
        nc.sync.dma_start(out=gb_stage[0:1, E:2 * E], in_=ln_beta.rearrange("(o e) -> o e", o=1))
        load_w(0)
        load_w(1)
        load_h(0)
        new_x(0)
        nc.sync.dma_start(out=xs[0][:, 0, :], in_=x_v[0][:, 0, :])
        load_h(1)
        nc.sync.dma_start(out=xs[0][:, 1, :], in_=x_v[0][:, 1, :])
        for r in range(1, NT // 2):
            load_h(2 * r)
            load_h(2 * r + 1)
            if r == 2:
                load_x(1)
            elif r > 3:
                load_x(r - 2)
        load_x(NT // 2 - 2)
        load_x(NT // 2 - 1)

        ones = const.tile([P, P], BF16, name="ones")
        nc.vector.memset(ones[:], 1.0)
        warm = const.tile([P, 1], F32, name="warm")
        nc.vector.memset(warm[:], 1.0)
        nc.vector.tensor_copy(out=gb_row[0:1, :], in_=gb_stage[0:1, :])
        warm2 = const.tile([P, 1], F32, name="warm2")
        nc.scalar.activation(out=warm2[:], in_=warm[:], func=ACT.Abs_reciprocal_sqrt)

        gam_ps = ps_gb.tile([P, E], BF16, name="gam_ps")
        bet_ps = ps_gb.tile([P, E], BF16, name="bet_ps")
        gam_sb = const.tile([P, E], BF16, name="gam_sb")
        bet_sb = const.tile([P, E], BF16, name="bet_sb")
        junk = const.tile([P, E], BF16, name="junk")
        junk2 = const.tile([P, 2], F32, name="junk2")
        w_codes = const.tile([P, 2, E], U32, name="w_codes", align_bytes=64)
        w_scales = const.tile([P, 2, E], U8, name="w_scales", align_bytes=64)

        def gb_bcast():
            for half in range(2):
                cols = slice(half * HALF, (half + 1) * HALF)
                nc.tensor.matmul(out=gam_ps[:, cols], lhsT=ones[:], rhs=gb_row[:, cols], start=True, stop=True)
            for half in range(2):
                cols = slice(half * HALF, (half + 1) * HALF)
                nc.tensor.matmul(out=bet_ps[:, cols], lhsT=ones[:], rhs=gb_row[:, E + half * HALF:E + (half + 1) * HALF],
                                 start=True, stop=True)

        def warm_pe(g):
            for row in range(4):
                nc.tensor.matmul(out=gam_ps[:, 0:HALF], lhsT=ones[:], rhs=w_raw[g][:, row, 0:HALF], start=True, stop=True)

        def gb_copy():
            nc.scalar.copy(out=gam_sb[:, CV_MAIN:E], in_=gam_ps[:, CV_MAIN:E])
            nc.scalar.copy(out=bet_sb[:, CV_MAIN:E], in_=bet_ps[:, CV_MAIN:E])

        w_grp = {}

        def wcopy(c):
            half, g = divmod(c, 2)
            grp = wgpool.tile([P, HALF, 4], BF16, name="w_grp", tag="w_grp", align_bytes=64)
            src = w_raw[g][:, :, half * HALF:(half + 1) * HALF].rearrange("p t n -> p n t")
            nc.vector.tensor_copy(out=grp[:, 0:WV, :], in_=src[:, 0:WV, :])
            nc.scalar.copy(out=grp[:, WV:HALF, :], in_=src[:, WV:HALF, :])
            w_grp[c] = grp

        def wq(c, pieces=1):
            half, g = divmod(c, 2)
            width = HALF // pieces
            for s in range(pieces):
                cols = slice(half * HALF + s * width, half * HALF + (s + 1) * width)
                nc.vector.quantize_mx(
                    out=w_codes[:, g, cols].bitcast(E5X4),
                    scales=w_scales[:, g, cols],
                    in_=w_grp[c][:, s * width:(s + 1) * width, :].rearrange("p n t -> p (n t)"),
                )

        m_grp = {}
        m_q = {}
        xts = {}

        def trp(i):
            if i >= NT:
                return
            words = hs[i][:].bitcast(F32)
            xt = ps_t.tile([P, HALF], F32, name="xt", tag="xt")
            for g in range(2):
                for u in range(2):
                    nc.tensor.transpose(
                        xt[:, (2 * g + u) * P:(2 * g + u + 1) * P],
                        words[:, 256 * g + u:256 * (g + 1):2],
                        ident[:],
                    )
            xts[i] = xt

        def cpo(i, on_vector=False):
            if i >= NT:
                return
            first, n = group_of(i)
            if i == first:
                grp = gpool.tile([P, 4 * E], BF16, name="m_grp", tag="m_grp", align_bytes=64)
                for s in range(n):
                    m_grp[first + s] = (grp, s)
            grp, s = m_grp[i]
            dst = grp[:, s * E:(s + 1) * E].bitcast(F32).rearrange("p (g r u) -> p g r u", g=2, u=2)
            src = xts[i][:].rearrange("p (g u r) -> p g r u", g=2, u=2)
            if on_vector:
                nc.vector.tensor_copy(out=dst, in_=src)
            else:
                nc.scalar.copy(out=dst, in_=src)

        def quant(i):
            first, n = group_of(i)
            mc = mqpool.tile([P, 4 * 256], U32, name="mc", tag="mc", align_bytes=64)
            ms = mqpool.tile([P, 4 * 256], U8, name="ms", tag="ms", align_bytes=64)
            grp = m_grp[i][0]
            nc.vector.quantize_mx(out=mc[:, 0:n * 256].bitcast(E5X4), scales=ms[:, 0:n * 256], in_=grp[:, 0:n * E])
            for s in range(n):
                m_q[i + s] = (mc, ms, s)

        accs = {}
        ys = {}
        os_ = {}
        sts = {}

        def mmh(i, half):
            mc, ms, s = m_q[i]
            acc = ps_acc.tile([P, HALF], F32, name="acc", tag="acc")
            cols = slice(half * HALF, (half + 1) * HALF)
            for g in range(2):
                mcols = slice(s * 256 + g * P, s * 256 + (g + 1) * P)
                nc.tensor.matmul_mx(
                    out=acc[:],
                    lhsT=mc[:, mcols].bitcast(E5X4),
                    lhsT_scale=ms[:, mcols],
                    rhs=w_codes[:, g, cols].bitcast(E5X4),
                    rhs_scale=w_scales[:, g, cols],
                    start=(g == 0),
                    stop=(g == 1),
                )
            accs[(i, half)] = acc

        def mm(i):
            mmh(i, 0)
            mmh(i, 1)

        def add_x(i, half):
            r, j = divmod(i, 2)
            if half == 0:
                ys[i] = ypool.tile([P, E], F32, name="y", tag="y")
                sts[i] = spool.tile([P, 8], F32, name="st", tag="st")
            cols = slice(half * HALF, (half + 1) * HALF)
            nc.vector.scalar_tensor_tensor(
                out=ys[i][:, cols], in0=accs[(i, half)][:], scalar=1.0, in1=xs[r][:, j, cols],
                op0=ALU.mult, op1=ALU.add, accum_out=sts[i][:, half:half + 1],
            )

        def negmean(i):
            st = sts[i]
            nc.scalar.activation(out=junk2[:], in_=st[:, 0:2], func=ACT.Identity, scale=-1.0 / E,
                                 accum_out=st[:, 2:3])

        def sumsq(i):
            st = sts[i]
            nc.scalar.activation(out=junk[:], in_=ys[i][:], func=ACT.Square, bias=st[:, 2:3], scale=1.0,
                                 accum_out=st[:, 3:4])

        def rstd(i):
            st = sts[i]
            nc.scalar.activation(out=st[:, 5:6], in_=st[:, 3:4], func=ACT.Abs_reciprocal_sqrt,
                                 scale=1.0 / E, bias=LN_EPS)

        def new_o(i):
            os_[i] = opool.tile([P, E], F32, name="o", tag="o")

        def nmr(i):
            st = sts[i]
            nc.scalar.activation(out=st[:, 6:7], in_=st[:, 2:3], func=ACT.Identity, scale=st[:, 5:6])

        def zs(i):
            st, o, cv = sts[i], os_[i], cv_of(i)
            nc.scalar.activation(out=o[:, cv:E], in_=ys[i][:, cv:E], func=ACT.Identity,
                                 scale=st[:, 5:6], bias=st[:, 6:7])

        def g1(i):
            o, cv = os_[i], cv_of(i)
            nc.gpsimd.tensor_tensor(out=o[:, cv:E], in0=o[:, cv:E], in1=gam_sb[:, cv:E], op=ALU.mult)

        def g2(i):
            o, cv = os_[i], cv_of(i)
            nc.gpsimd.tensor_tensor(out=o[:, cv:E], in0=o[:, cv:E], in1=bet_sb[:, cv:E], op=ALU.add)

        def t1(i):
            o, cv = os_[i], cv_of(i)
            nc.vector.scalar_tensor_tensor(
                out=o[:, 0:cv], in0=ys[i][:, 0:cv], scalar=sts[i][:, 2:3], in1=gam_ps[:, 0:cv],
                op0=ALU.add, op1=ALU.mult,
            )

        def t2(i, c0, c1):
            o = os_[i]
            nc.vector.scalar_tensor_tensor(
                out=o[:, c0:c1], in0=o[:, c0:c1], scalar=sts[i][:, 5:6], in1=bet_ps[:, c0:c1],
                op0=ALU.mult, op1=ALU.add,
            )

        def store(i, c0, c1):
            r, j = divmod(i, 2)
            nc.sync.dma_start(out=o_v[r][:, j, c0:c1], in_=os_[i][:, c0:c1])

        warm_pe(0)
        wcopy(0)
        wcopy(2)
        wq(0)
        wq(2)
        warm_pe(1)
        wcopy(1)
        wcopy(3)
        wq(1)
        trp(0)
        gb_bcast()
        cpo(0)
        quant(0)
        trp(1)
        mmh(0, 0)
        cpo(1)
        gb_copy()
        wq(3)
        add_x(0, 0)
        quant(1)
        mmh(0, 1)
        trp(2)
        mm(1)
        trp(3)
        cpo(2)
        add_x(0, 1)
        negmean(0)
        sumsq(0)
        cpo(3)
        new_o(0)
        add_x(1, 0)
        add_x(1, 1)
        t1(0)
        quant(2)
        trp(4)
        mm(2)
        trp(5)
        mm(3)
        rstd(0)
        nmr(0)
        zs(0)
        g1(0)
        negmean(1)
        new_o(1)
        t1(1)
        t2(0, 0, cv_of(0))
        sumsq(1)
        cpo(4)
        rstd(1)
        cpo(5)

        for k in range(2, NT + 2):
            if k < NT:
                add_x(k, 0)
                add_x(k, 1)
                negmean(k)
                new_o(k)
            trp(k + LOOK)
            cpo(k + LOOK)
            if k + 2 < NT and group_of(k + 2)[0] == k + 2:
                quant(k + 2)
            if k - 1 < NT and cv_of(k - 1) < E:
                nmr(k - 1)
            if k < NT:
                sumsq(k)
            if k - 1 < NT and cv_of(k - 1) < E:
                zs(k - 1)
            if k < NT:
                rstd(k)
            if k - 2 < NT and cv_of(k - 2) < E:
                g2(k - 2)
            if k - 1 < NT and cv_of(k - 1) < E:
                g1(k - 1)
            if k - 2 == NT - 1:
                t2(k - 2, 0, HALF)
                store(k - 2, 0, HALF)
                t2(k - 2, HALF, E)
                store(k - 2, HALF, E)
            else:
                if k - 1 == NT - 1:
                    t1(k - 1)
                if k >= 3:
                    t2(k - 2, 0, cv_of(k - 2))
                store(k - 2, 0, E)
            if k >= 3 and k - 1 < NT - 1:
                t1(k - 1)
            if k + 2 < NT:
                mm(k + 2)
